import numpy as np
import ml_dtypes


def mxq(x, axis, fmt="e4m3"):
    dtype, down = {"e4m3": (ml_dtypes.float8_e4m3fn, 7), "e5m2": (ml_dtypes.float8_e5m2, 14)}[fmt]
    v = np.moveaxis(np.asarray(x, np.float32).astype(ml_dtypes.bfloat16).astype(np.float64), axis, -1)
    blocks = v.reshape(v.shape[:-1] + (-1, 32))
    amax = np.abs(blocks).max(-1, keepdims=True)
    byte = np.maximum(np.where(amax > 0, np.frexp(amax)[1] - 1 + 127, 0) - down, 1)
    scale = np.exp2(byte - 127.0)
    codes = (blocks / scale).astype(np.float32).astype(dtype).astype(np.float64)
    return np.moveaxis((codes * scale).reshape(v.shape), -1, axis)


WIDE = False


def mx_kscale(k):
    if not WIDE:
        return np.ones(k)
    levels = np.array([10, -10, 5, -5, 0])
    a = np.random.permutation(np.resize(levels, k // 512 * 4)).reshape(k // 512, 4)
    idx = np.arange(k)
    return np.exp2(a[idx // 512, idx % 128 // 32])


BF16 = ml_dtypes.bfloat16


def bf(x):
    return np.asarray(x, np.float32).astype(BF16)


def f64(x):
    return np.asarray(x).astype(np.float64)


E2M1 = np.array([0.0, 0.5, 1.0, 1.5, 2.0, 3.0, 4.0, 6.0, -0.0, -0.5, -1.0, -1.5, -2.0, -3.0, -4.0, -6.0])


def pack_weight(w, fmt):
    k, n = w.shape
    w = f64(bf(w)).reshape(k // 32, 32, n)
    amax = np.abs(w).max(1)
    if fmt == "e4m3":
        byte = np.frexp(amax)[1] - 1 + 127 - 7
    else:
        mant, ex = np.frexp(amax / 6.0)
        byte = np.where(mant > 0.5, ex, ex - 1) + 127
    byte = np.clip(np.where(amax > 0, byte, 1), 1, 254)
    scaled = (w * np.exp2(127.0 - byte)[:, None, :]).reshape(k, n).astype(np.float32)
    by_word = np.ascontiguousarray(scaled.reshape(k // 512, 128, 4, n).transpose(0, 1, 3, 2))
    if fmt == "e4m3":
        words = by_word.astype(ml_dtypes.float8_e4m3fn).view(np.uint8)
    else:
        c = by_word.astype(ml_dtypes.float4_e2m1fn).view(np.uint8) & 0xF
        words = c[..., 0::2] | (c[..., 1::2] << 4)
    return np.ascontiguousarray(words), np.ascontiguousarray(byte.astype(np.uint8).reshape(k // 512, 16, n))


def unpack_weight(words, scales, fmt):
    g, p, n, _ = words.shape
    if fmt == "e4m3":
        vals = np.ascontiguousarray(words).view(ml_dtypes.float8_e4m3fn).astype(np.float64)
    else:
        nib = np.empty((g, p, n, 4), np.uint8)
        nib[..., 0::2] = words & 0xF
        nib[..., 1::2] = words >> 4
        vals = E2M1[nib]
    vals = vals * np.repeat(np.exp2(scales.astype(np.float64) - 127.0), 8, axis=1)[..., None]
    return vals.transpose(0, 1, 3, 2).reshape(g * 512, n)


B, C, H, W = 16, 512, 16, 32
HW = H * W


def setup_inputs():
    s = mx_kscale(C)
    x = bf(np.random.standard_normal((B, C, H, W)) * s[None, :, None, None])
    m = bf(0.5 * HW / B + np.random.standard_normal((B, HW)))
    w_mask = np.random.standard_normal((C, C)) * 0.5 * HW / np.sqrt(C) / s[None, :]
    words, scales = pack_weight(np.ascontiguousarray(w_mask.T), "e4m3")
    return {"x": x, "m": m, "w_mask_words": words, "w_mask_scales": scales}


def reference(x, m, w_mask_words, w_mask_scales):
    mm = f64(m)
    e = np.exp(mm - mm.max(axis=-1, keepdims=True))
    attn = (e / e.sum(axis=-1, keepdims=True)).reshape(B, 1, H, W)
    gated = (f64(x) * attn).reshape(B, C, HW)
    y = unpack_weight(w_mask_words, w_mask_scales, "e4m3").T @ mxq(gated, 1, "e4m3")
    return y.reshape(B, C, H, W)

@@ -1,0 +1,131 @@
+from contextlib import ExitStack
+
+import concourse.mybir as mybir
+from concourse.masks import make_identity
+
+F32 = mybir.dt.float32
+BF16 = mybir.dt.bfloat16
+I32 = mybir.dt.int32
+U32 = mybir.dt.uint32
+U8 = mybir.dt.uint8
+FP8X4 = mybir.dt.float8_e4m3fn_x4
+
+P = 128
+PACK = 4
+IMAGES = 16
+CHANNELS = P * PACK
+PIXELS = 512
+OUT_BLOCKS = CHANNELS // P
+
+FLOPS = 2 * IMAGES * CHANNELS * CHANNELS * PIXELS
+
+
+def load_weight(nc, keep, w_mask_words, w_mask_scales):
+    w_codes = keep.tile([P, CHANNELS], U32, align_bytes=64)
+    w_scales = keep.tile([P, CHANNELS], U8, align_bytes=64)
+    nc.vector.memset(w_scales[:].bitcast(I32), 0)
+    for quadrant in range(4):
+        nc.sync.dma_start(
+            out=w_scales[32 * quadrant : 32 * quadrant + 4, :].bitcast(I32),
+            in_=w_mask_scales[0, 4 * quadrant : 4 * quadrant + 4, :].bitcast(I32),
+        )
+    nc.sync.dma_start(
+        out=w_codes[:].bitcast(I32),
+        in_=w_mask_words[0].rearrange("p n t -> p (n t)").bitcast(I32),
+    )
+    return w_codes, w_scales
+
+
+def softmax_rows(nc, keep, m_rows):
+    row_max = keep.tile([IMAGES, 1], F32)
+    nc.vector.reduce_max(out=row_max[:], in_=m_rows[:], axis=mybir.AxisListType.X)
+    minus_max = keep.tile([IMAGES, 1], F32)
+    nc.vector.tensor_scalar_mul(out=minus_max[:], in0=row_max[:], scalar1=-1.0)
+    exps = keep.tile([IMAGES, PIXELS], F32)
+    exp_sum = keep.tile([IMAGES, 1], F32)
+    nc.scalar.activation(
+        out=exps[:],
+        in_=m_rows[:],
+        func=mybir.ActivationFunctionType.Exp,
+        bias=minus_max[:],
+        scale=1.0,
+        accum_out=exp_sum[:],
+    )
+    inv_sum = keep.tile([IMAGES, 1], F32)
+    nc.vector.reciprocal(out=inv_sum[:], in_=exp_sum[:])
+    attn = keep.tile([P, PIXELS], F32)
+    nc.vector.memset(attn[:], 0.0)
+    nc.vector.tensor_scalar_mul(out=attn[0:IMAGES, :], in0=exps[:], scalar1=inv_sum[:])
+    return attn
+
+
+def tile_nlgp_pb_t_kernel(tc, x, m, w_mask_words, w_mask_scales, out):
+    nc = tc.nc
+    with ExitStack() as ctx:
+        keep = ctx.enter_context(tc.tile_pool(name="keep", bufs=1))
+        x_pool = ctx.enter_context(tc.tile_pool(name="x_pool", bufs=IMAGES))
+        y_pool = ctx.enter_context(tc.tile_pool(name="y_pool", bufs=3))
+        out_pool = ctx.enter_context(tc.tile_pool(name="out_pool", bufs=6))
+        gate_psum = ctx.enter_context(tc.psum_pool(name="gate_psum", bufs=3))
+        acc_psum = ctx.enter_context(tc.psum_pool(name="acc_psum", bufs=5))
+
+        m_rows = keep.tile([IMAGES, PIXELS], BF16)
+        nc.sync.dma_start(out=m_rows[:], in_=m)
+        x_images = []
+        for b in range(IMAGES):
+            x_image = x_pool.tile([P, PACK, PIXELS], BF16)
+            nc.sync.dma_start(
+                out=x_image[:].rearrange("p t n -> p (t n)"),
+                in_=x[b].rearrange("(p t) h w -> p (t h w)", t=PACK),
+            )
+            x_images.append(x_image)
+            if b == 0:
+                w_codes, w_scales = load_weight(nc, keep, w_mask_words, w_mask_scales)
+
+        identity = keep.tile([P, P], F32)
+        make_identity(nc, identity[:])
+        attn = softmax_rows(nc, keep, m_rows)
+
+        for b in range(IMAGES):
+            gate = gate_psum.tile([P, PIXELS], F32)
+            nc.tensor.matmul(
+                out=gate[:],
+                lhsT=identity[:, b : b + 1].to_broadcast([P, P]),
+                rhs=attn[:],
+                start=True,
+                stop=True,
+            )
+
+            y = y_pool.tile([P, PIXELS, PACK], BF16, align_bytes=64)
+            nc.vector.tensor_tensor(
+                out=y[:],
+                in0=x_images[b][:].rearrange("p t n -> p n t"),
+                in1=gate[:].unsqueeze(2).to_broadcast([P, PIXELS, PACK]),
+                op=mybir.AluOpType.mult,
+            )
+            y_codes = y_pool.tile([P, PIXELS], U32, align_bytes=64)
+            y_scales = y_pool.tile([P, PIXELS], U8, align_bytes=64)
+            nc.vector.quantize_mx(
+                out=y_codes[:].bitcast(FP8X4),
+                scales=y_scales[:],
+                in_=y[:].rearrange("p n t -> p (n t)"),
+            )
+
+            out_image = out_pool.tile([P, OUT_BLOCKS, PIXELS], F32)
+            for block in range(OUT_BLOCKS):
+                d_cols = slice(block * P, (block + 1) * P)
+                acc = acc_psum.tile([P, PIXELS], F32)
+                nc.tensor.matmul_mx(
+                    out=acc[:],
+                    lhsT=w_codes[:, d_cols].bitcast(FP8X4),
+                    lhsT_scale=w_scales[:, d_cols],
+                    rhs=y_codes[:].bitcast(FP8X4),
+                    rhs_scale=y_scales[:],
+                    start=True,
+                    stop=True,
+                )
+                nc.scalar.copy(out=out_image[:, block, :], in_=acc[:])
+            nc.sync.dma_start(
+                out=out[b].rearrange("(k p) h w -> p k (h w)", p=P),
+                in_=out_image[:],
+            )

@@ -16,6 +16,7 @@ IMAGES = 16
 CHANNELS = P * PACK
 PIXELS = 512
 OUT_BLOCKS = CHANNELS // P
+GATES_AHEAD = 3
 
 FLOPS = 2 * IMAGES * CHANNELS * CHANNELS * PIXELS
 
@@ -37,6 +38,8 @@ def load_weight(nc, keep, w_mask_words, w_mask_scales):
 
 
 def softmax_rows(nc, keep, m_rows):
+    attn = keep.tile([P, PIXELS], F32)
+    nc.vector.memset(attn[:], 0.0)
     row_max = keep.tile([IMAGES, 1], F32)
     nc.vector.reduce_max(out=row_max[:], in_=m_rows[:], axis=mybir.AxisListType.X)
     minus_max = keep.tile([IMAGES, 1], F32)
@@ -53,8 +56,6 @@ def softmax_rows(nc, keep, m_rows):
     )
     inv_sum = keep.tile([IMAGES, 1], F32)
     nc.vector.reciprocal(out=inv_sum[:], in_=exp_sum[:])
-    attn = keep.tile([P, PIXELS], F32)
-    nc.vector.memset(attn[:], 0.0)
     nc.vector.tensor_scalar_mul(out=attn[0:IMAGES, :], in0=exps[:], scalar1=inv_sum[:])
     return attn
 
@@ -62,12 +63,13 @@ def softmax_rows(nc, keep, m_rows):
 def tile_nlgp_pb_t_kernel(tc, x, m, w_mask_words, w_mask_scales, out):
     nc = tc.nc
     with ExitStack() as ctx:
+        ctx.enter_context(tc.manual_schedule())
         keep = ctx.enter_context(tc.tile_pool(name="keep", bufs=1))
         x_pool = ctx.enter_context(tc.tile_pool(name="x_pool", bufs=IMAGES))
         y_pool = ctx.enter_context(tc.tile_pool(name="y_pool", bufs=3))
         out_pool = ctx.enter_context(tc.tile_pool(name="out_pool", bufs=6))
-        gate_psum = ctx.enter_context(tc.psum_pool(name="gate_psum", bufs=3))
-        acc_psum = ctx.enter_context(tc.psum_pool(name="acc_psum", bufs=5))
+        gate_psum = ctx.enter_context(tc.psum_pool(name="gate_psum", bufs=GATES_AHEAD))
+        acc_psum = ctx.enter_context(tc.psum_pool(name="acc_psum", bufs=8 - GATES_AHEAD))
 
         m_rows = keep.tile([IMAGES, PIXELS], BF16)
         nc.sync.dma_start(out=m_rows[:], in_=m)
@@ -86,7 +88,10 @@ def tile_nlgp_pb_t_kernel(tc, x, m, w_mask_words, w_mask_scales, out):
         make_identity(nc, identity[:])
         attn = softmax_rows(nc, keep, m_rows)
 
-        for b in range(IMAGES):
+        gates = {}
+        products = {}
+
+        def spread_gate(b):
             gate = gate_psum.tile([P, PIXELS], F32)
             nc.tensor.matmul(
                 out=gate[:],
@@ -95,22 +100,26 @@ def tile_nlgp_pb_t_kernel(tc, x, m, w_mask_words, w_mask_scales, out):
                 start=True,
                 stop=True,
             )
+            gates[b] = gate
 
+        def multiply(b):
             y = y_pool.tile([P, PIXELS, PACK], BF16, align_bytes=64)
             nc.vector.tensor_tensor(
                 out=y[:],
                 in0=x_images[b][:].rearrange("p t n -> p n t"),
-                in1=gate[:].unsqueeze(2).to_broadcast([P, PIXELS, PACK]),
+                in1=gates[b][:].unsqueeze(2).to_broadcast([P, PIXELS, PACK]),
                 op=mybir.AluOpType.mult,
             )
+            products[b] = y
+
+        def convolve(b):
             y_codes = y_pool.tile([P, PIXELS], U32, align_bytes=64)
             y_scales = y_pool.tile([P, PIXELS], U8, align_bytes=64)
             nc.vector.quantize_mx(
                 out=y_codes[:].bitcast(FP8X4),
                 scales=y_scales[:],
-                in_=y[:].rearrange("p n t -> p (n t)"),
+                in_=products[b][:].rearrange("p n t -> p (n t)"),
             )
-
             out_image = out_pool.tile([P, OUT_BLOCKS, PIXELS], F32)
             for block in range(OUT_BLOCKS):
                 d_cols = slice(block * P, (block + 1) * P)
@@ -129,3 +138,13 @@ def tile_nlgp_pb_t_kernel(tc, x, m, w_mask_words, w_mask_scales, out):
                 out=out[b].rearrange("(k p) h w -> p k (h w)", p=P),
                 in_=out_image[:],
             )
+
+        for b in range(GATES_AHEAD):
+            spread_gate(b)
+        multiply(0)
+        for b in range(IMAGES):
+            if b + GATES_AHEAD < IMAGES:
+                spread_gate(b + GATES_AHEAD)
+            if b + 1 < IMAGES:
+                multiply(b + 1)
+            convolve(b)

@@ -17,6 +17,7 @@ CHANNELS = P * PACK
 PIXELS = 512
 OUT_BLOCKS = CHANNELS // P
 GATES_AHEAD = 3
+RUN = 4
 
 FLOPS = 2 * IMAGES * CHANNELS * CHANNELS * PIXELS
 
@@ -67,22 +68,32 @@ def tile_nlgp_pb_t_kernel(tc, x, m, w_mask_words, w_mask_scales, out):
         keep = ctx.enter_context(tc.tile_pool(name="keep", bufs=1))
         x_pool = ctx.enter_context(tc.tile_pool(name="x_pool", bufs=IMAGES))
         y_pool = ctx.enter_context(tc.tile_pool(name="y_pool", bufs=3))
-        out_pool = ctx.enter_context(tc.tile_pool(name="out_pool", bufs=6))
+        out_pool = ctx.enter_context(tc.tile_pool(name="out_pool", bufs=4 * OUT_BLOCKS))
         gate_psum = ctx.enter_context(tc.psum_pool(name="gate_psum", bufs=GATES_AHEAD))
         acc_psum = ctx.enter_context(tc.psum_pool(name="acc_psum", bufs=8 - GATES_AHEAD))
 
-        m_rows = keep.tile([IMAGES, PIXELS], BF16)
-        nc.sync.dma_start(out=m_rows[:], in_=m)
+        scratch = keep.tile([P, 2], F32)
+        nc.vector.memset(scratch[:], 0.0)
+        nc.scalar.activation(
+            out=scratch[:, 1:2], in_=scratch[:, 0:1], func=mybir.ActivationFunctionType.Exp
+        )
+
         x_images = []
-        for b in range(IMAGES):
+
+        def load_image(b):
             x_image = x_pool.tile([P, PACK, PIXELS], BF16)
             nc.sync.dma_start(
                 out=x_image[:].rearrange("p t n -> p (t n)"),
                 in_=x[b].rearrange("(p t) h w -> p (t h w)", t=PACK),
             )
             x_images.append(x_image)
-            if b == 0:
-                w_codes, w_scales = load_weight(nc, keep, w_mask_words, w_mask_scales)
+
+        m_rows = keep.tile([IMAGES, PIXELS], BF16)
+        nc.sync.dma_start(out=m_rows[:], in_=m)
+        load_image(0)
+        w_codes, w_scales = load_weight(nc, keep, w_mask_words, w_mask_scales)
+        for b in range(1, IMAGES):
+            load_image(b)
 
         identity = keep.tile([P, P], F32)
         make_identity(nc, identity[:])
@@ -105,9 +116,12 @@ def tile_nlgp_pb_t_kernel(tc, x, m, w_mask_words, w_mask_scales, out):
         def multiply(b):
             y = y_pool.tile([P, PIXELS, PACK], BF16, align_bytes=64)
             nc.vector.tensor_tensor(
-                out=y[:],
-                in0=x_images[b][:].rearrange("p t n -> p n t"),
-                in1=gates[b][:].unsqueeze(2).to_broadcast([P, PIXELS, PACK]),
+                out=y[:].rearrange("p (c i) t -> p c t i", i=RUN),
+                in0=x_images[b][:].rearrange("p t (c i) -> p c t i", i=RUN),
+                in1=gates[b][:]
+                .rearrange("p (c i) -> p c i", i=RUN)
+                .unsqueeze(2)
+                .to_broadcast([P, PIXELS // RUN, PACK, RUN]),
                 op=mybir.AluOpType.mult,
             )
             products[b] = y
@@ -120,7 +134,6 @@ def tile_nlgp_pb_t_kernel(tc, x, m, w_mask_words, w_mask_scales, out):
                 scales=y_scales[:],
                 in_=products[b][:].rearrange("p n t -> p (n t)"),
             )
-            out_image = out_pool.tile([P, OUT_BLOCKS, PIXELS], F32)
             for block in range(OUT_BLOCKS):
                 d_cols = slice(block * P, (block + 1) * P)
                 acc = acc_psum.tile([P, PIXELS], F32)
@@ -133,11 +146,11 @@ def tile_nlgp_pb_t_kernel(tc, x, m, w_mask_words, w_mask_scales, out):
                     start=True,
                     stop=True,
                 )
-                nc.scalar.copy(out=out_image[:, block, :], in_=acc[:])
-            nc.sync.dma_start(
-                out=out[b].rearrange("(k p) h w -> p k (h w)", p=P),
-                in_=out_image[:],
-            )
+                out_block = out_pool.tile([P, PIXELS], F32)
+                nc.scalar.copy(out=out_block[:], in_=acc[:])
+                nc.sync.dma_start(
+                    out=out[b, d_cols].rearrange("p h w -> p (h w)"), in_=out_block[:]
+                )
 
         for b in range(GATES_AHEAD):
             spread_gate(b)

@@ -17,7 +17,7 @@ CHANNELS = P * PACK
 PIXELS = 512
 OUT_BLOCKS = CHANNELS // P
 GATES_AHEAD = 3
-RUN = 4
+RUN = 1
 
 FLOPS = 2 * IMAGES * CHANNELS * CHANNELS * PIXELS
 

@@ -17,7 +17,7 @@ CHANNELS = P * PACK
 PIXELS = 512
 OUT_BLOCKS = CHANNELS // P
 GATES_AHEAD = 3
-RUN = 1
+RUN = 4
 
 FLOPS = 2 * IMAGES * CHANNELS * CHANNELS * PIXELS
 
@@ -147,7 +147,10 @@ def tile_nlgp_pb_t_kernel(tc, x, m, w_mask_words, w_mask_scales, out):
                     stop=True,
                 )
                 out_block = out_pool.tile([P, PIXELS], F32)
-                nc.scalar.copy(out=out_block[:], in_=acc[:])
+                if b == IMAGES - 1:
+                    nc.vector.tensor_copy(out=out_block[:], in_=acc[:])
+                else:
+                    nc.scalar.copy(out=out_block[:], in_=acc[:])
                 nc.sync.dma_start(
                     out=out[b, d_cols].rearrange("p h w -> p (h w)"), in_=out_block[:]
                 )

@@ -18,6 +18,8 @@ PIXELS = 512
 OUT_BLOCKS = CHANNELS // P
 GATES_AHEAD = 3
 RUN = 4
+GPSIMD_PIXELS = 128
+VECTOR_PIXELS = PIXELS - GPSIMD_PIXELS
 
 FLOPS = 2 * IMAGES * CHANNELS * CHANNELS * PIXELS
 
@@ -69,6 +71,7 @@ def tile_nlgp_pb_t_kernel(tc, x, m, w_mask_words, w_mask_scales, out):
         x_pool = ctx.enter_context(tc.tile_pool(name="x_pool", bufs=IMAGES))
         y_pool = ctx.enter_context(tc.tile_pool(name="y_pool", bufs=3))
         out_pool = ctx.enter_context(tc.tile_pool(name="out_pool", bufs=4 * OUT_BLOCKS))
+        gate_pool = ctx.enter_context(tc.tile_pool(name="gate_pool", bufs=GATES_AHEAD + 1))
         gate_psum = ctx.enter_context(tc.psum_pool(name="gate_psum", bufs=GATES_AHEAD))
         acc_psum = ctx.enter_context(tc.psum_pool(name="acc_psum", bufs=8 - GATES_AHEAD))
 
@@ -100,6 +103,7 @@ def tile_nlgp_pb_t_kernel(tc, x, m, w_mask_words, w_mask_scales, out):
         attn = softmax_rows(nc, keep, m_rows)
 
         gates = {}
+        gate_copies = {}
         products = {}
 
         def spread_gate(b):
@@ -112,16 +116,25 @@ def tile_nlgp_pb_t_kernel(tc, x, m, w_mask_words, w_mask_scales, out):
                 stop=True,
             )
             gates[b] = gate
+            gate_copy = gate_pool.tile([P, GPSIMD_PIXELS], F32)
+            nc.scalar.copy(out=gate_copy[:], in_=gate[:, VECTOR_PIXELS:PIXELS])
+            gate_copies[b] = gate_copy
 
         def multiply(b):
             y = y_pool.tile([P, PIXELS, PACK], BF16, align_bytes=64)
             nc.vector.tensor_tensor(
-                out=y[:].rearrange("p (c i) t -> p c t i", i=RUN),
-                in0=x_images[b][:].rearrange("p t (c i) -> p c t i", i=RUN),
-                in1=gates[b][:]
+                out=y[:, 0:VECTOR_PIXELS, :].rearrange("p (c i) t -> p c t i", i=RUN),
+                in0=x_images[b][:, :, 0:VECTOR_PIXELS].rearrange("p t (c i) -> p c t i", i=RUN),
+                in1=gates[b][:, 0:VECTOR_PIXELS]
                 .rearrange("p (c i) -> p c i", i=RUN)
                 .unsqueeze(2)
-                .to_broadcast([P, PIXELS // RUN, PACK, RUN]),
+                .to_broadcast([P, VECTOR_PIXELS // RUN, PACK, RUN]),
+                op=mybir.AluOpType.mult,
+            )
+            nc.gpsimd.tensor_tensor(
+                out=y[:, VECTOR_PIXELS:PIXELS, :],
+                in0=x_images[b][:, :, VECTOR_PIXELS:PIXELS].rearrange("p t n -> p n t"),
+                in1=gate_copies[b][:].unsqueeze(2).to_broadcast([P, GPSIMD_PIXELS, PACK]),
                 op=mybir.AluOpType.mult,
             )
             products[b] = y

@@ -40,6 +40,20 @@ def load_weight(nc, keep, w_mask_words, w_mask_scales):
     return w_codes, w_scales
 
 
+def group_output_channels(nc, keep, w_codes, w_scales):
+    codes = keep.tile([P, CHANNELS], U32, align_bytes=64)
+    scales = keep.tile([P, CHANNELS], U8, align_bytes=64)
+    nc.gpsimd.tensor_copy(
+        out=codes[:].rearrange("p (j m) -> p m j", j=OUT_BLOCKS),
+        in_=w_codes[:].rearrange("p (m j) -> p m j", j=OUT_BLOCKS),
+    )
+    nc.gpsimd.tensor_copy(
+        out=scales[:].rearrange("p (j m) -> p m j", j=OUT_BLOCKS),
+        in_=w_scales[:].rearrange("p (m j) -> p m j", j=OUT_BLOCKS),
+    )
+    return codes, scales
+
+
 def softmax_rows(nc, keep, m_rows):
     attn = keep.tile([P, PIXELS], F32)
     nc.vector.memset(attn[:], 0.0)
@@ -70,7 +84,7 @@ def tile_nlgp_pb_t_kernel(tc, x, m, w_mask_words, w_mask_scales, out):
         keep = ctx.enter_context(tc.tile_pool(name="keep", bufs=1))
         x_pool = ctx.enter_context(tc.tile_pool(name="x_pool", bufs=IMAGES))
         y_pool = ctx.enter_context(tc.tile_pool(name="y_pool", bufs=3))
-        out_pool = ctx.enter_context(tc.tile_pool(name="out_pool", bufs=4 * OUT_BLOCKS))
+        out_pool = ctx.enter_context(tc.tile_pool(name="out_pool", bufs=4))
         gate_pool = ctx.enter_context(tc.tile_pool(name="gate_pool", bufs=GATES_AHEAD + 1))
         gate_psum = ctx.enter_context(tc.psum_pool(name="gate_psum", bufs=GATES_AHEAD))
         acc_psum = ctx.enter_context(tc.psum_pool(name="acc_psum", bufs=8 - GATES_AHEAD))
@@ -100,6 +114,7 @@ def tile_nlgp_pb_t_kernel(tc, x, m, w_mask_words, w_mask_scales, out):
 
         identity = keep.tile([P, P], F32)
         make_identity(nc, identity[:])
+        w_codes, w_scales = group_output_channels(nc, keep, w_codes, w_scales)
         attn = softmax_rows(nc, keep, m_rows)
 
         gates = {}
@@ -147,6 +162,9 @@ def tile_nlgp_pb_t_kernel(tc, x, m, w_mask_words, w_mask_scales, out):
                 scales=y_scales[:],
                 in_=products[b][:].rearrange("p n t -> p (n t)"),
             )
+            last = b == IMAGES - 1
+            out_rows = out[b].rearrange("(m j) h w -> m j (h w)", j=OUT_BLOCKS)
+            out_image = out_pool.tile([P, OUT_BLOCKS, PIXELS], F32)
             for block in range(OUT_BLOCKS):
                 d_cols = slice(block * P, (block + 1) * P)
                 acc = acc_psum.tile([P, PIXELS], F32)
@@ -159,14 +177,13 @@ def tile_nlgp_pb_t_kernel(tc, x, m, w_mask_words, w_mask_scales, out):
                     start=True,
                     stop=True,
                 )
-                out_block = out_pool.tile([P, PIXELS], F32)
-                if b == IMAGES - 1:
-                    nc.vector.tensor_copy(out=out_block[:], in_=acc[:])
+                if last:
+                    nc.vector.tensor_copy(out=out_image[:, block, :], in_=acc[:])
+                    nc.sync.dma_start(out=out_rows[:, block, :], in_=out_image[:, block, :])
                 else:
-                    nc.scalar.copy(out=out_block[:], in_=acc[:])
-                nc.sync.dma_start(
-                    out=out[b, d_cols].rearrange("p h w -> p (h w)"), in_=out_block[:]
-                )
+                    nc.scalar.copy(out=out_image[:, block, :], in_=acc[:])
+            if not last:
+                nc.sync.dma_start(out=out_rows, in_=out_image[:])
 
         for b in range(GATES_AHEAD):
             spread_gate(b)

@@ -20,6 +20,7 @@ GATES_AHEAD = 3
 RUN = 4
 GPSIMD_PIXELS = 128
 VECTOR_PIXELS = PIXELS - GPSIMD_PIXELS
+OUT_IMAGES = 10
 
 FLOPS = 2 * IMAGES * CHANNELS * CHANNELS * PIXELS
 
@@ -84,7 +85,7 @@ def tile_nlgp_pb_t_kernel(tc, x, m, w_mask_words, w_mask_scales, out):
         keep = ctx.enter_context(tc.tile_pool(name="keep", bufs=1))
         x_pool = ctx.enter_context(tc.tile_pool(name="x_pool", bufs=IMAGES))
         y_pool = ctx.enter_context(tc.tile_pool(name="y_pool", bufs=3))
-        out_pool = ctx.enter_context(tc.tile_pool(name="out_pool", bufs=4))
+        out_pool = ctx.enter_context(tc.tile_pool(name="out_pool", bufs=OUT_IMAGES))
         gate_pool = ctx.enter_context(tc.tile_pool(name="gate_pool", bufs=GATES_AHEAD + 1))
         gate_psum = ctx.enter_context(tc.psum_pool(name="gate_psum", bufs=GATES_AHEAD))
         acc_psum = ctx.enter_context(tc.psum_pool(name="acc_psum", bufs=8 - GATES_AHEAD))

@@ -18,9 +18,8 @@ PIXELS = 512
 OUT_BLOCKS = CHANNELS // P
 GATES_AHEAD = 3
 RUN = 4
-GPSIMD_PIXELS = 128
+GPSIMD_PIXELS = 96
 VECTOR_PIXELS = PIXELS - GPSIMD_PIXELS
-OUT_IMAGES = 10
 
 FLOPS = 2 * IMAGES * CHANNELS * CHANNELS * PIXELS
 
@@ -85,7 +84,7 @@ def tile_nlgp_pb_t_kernel(tc, x, m, w_mask_words, w_mask_scales, out):
         keep = ctx.enter_context(tc.tile_pool(name="keep", bufs=1))
         x_pool = ctx.enter_context(tc.tile_pool(name="x_pool", bufs=IMAGES))
         y_pool = ctx.enter_context(tc.tile_pool(name="y_pool", bufs=3))
-        out_pool = ctx.enter_context(tc.tile_pool(name="out_pool", bufs=OUT_IMAGES))
+        out_pool = ctx.enter_context(tc.tile_pool(name="out_pool", bufs=IMAGES))
         gate_pool = ctx.enter_context(tc.tile_pool(name="gate_pool", bufs=GATES_AHEAD + 1))
         gate_psum = ctx.enter_context(tc.psum_pool(name="gate_psum", bufs=GATES_AHEAD))
         acc_psum = ctx.enter_context(tc.psum_pool(name="acc_psum", bufs=8 - GATES_AHEAD))
@@ -180,11 +179,9 @@ def tile_nlgp_pb_t_kernel(tc, x, m, w_mask_words, w_mask_scales, out):
                 )
                 if last:
                     nc.vector.tensor_copy(out=out_image[:, block, :], in_=acc[:])
-                    nc.sync.dma_start(out=out_rows[:, block, :], in_=out_image[:, block, :])
                 else:
                     nc.scalar.copy(out=out_image[:, block, :], in_=acc[:])
-            if not last:
-                nc.sync.dma_start(out=out_rows, in_=out_image[:])
+            nc.sync.dma_start(out=out_rows, in_=out_image[:])
 
         for b in range(GATES_AHEAD):
             spread_gate(b)

@@ -17,6 +17,8 @@ CHANNELS = P * PACK
 PIXELS = 512
 OUT_BLOCKS = CHANNELS // P
 GATES_AHEAD = 3
+LOADS = [(0, 1), (1, 1), (2, 2), (4, 4), (8, 4), (12, 4)]
+LAST_STORES = 2
 RUN = 4
 GPSIMD_PIXELS = 96
 VECTOR_PIXELS = PIXELS - GPSIMD_PIXELS
@@ -29,7 +31,7 @@ def load_weight(nc, keep, w_mask_words, w_mask_scales):
     w_scales = keep.tile([P, CHANNELS], U8, align_bytes=64)
     nc.vector.memset(w_scales[:].bitcast(I32), 0)
     for quadrant in range(4):
-        nc.sync.dma_start(
+        nc.scalar.dma_start(
             out=w_scales[32 * quadrant : 32 * quadrant + 4, :].bitcast(I32),
             in_=w_mask_scales[0, 4 * quadrant : 4 * quadrant + 4, :].bitcast(I32),
         )
@@ -82,7 +84,7 @@ def tile_nlgp_pb_t_kernel(tc, x, m, w_mask_words, w_mask_scales, out):
     with ExitStack() as ctx:
         ctx.enter_context(tc.manual_schedule())
         keep = ctx.enter_context(tc.tile_pool(name="keep", bufs=1))
-        x_pool = ctx.enter_context(tc.tile_pool(name="x_pool", bufs=IMAGES))
+        x_pool = ctx.enter_context(tc.tile_pool(name="x_pool", bufs=1))
         y_pool = ctx.enter_context(tc.tile_pool(name="y_pool", bufs=3))
         out_pool = ctx.enter_context(tc.tile_pool(name="out_pool", bufs=IMAGES))
         gate_pool = ctx.enter_context(tc.tile_pool(name="gate_pool", bufs=GATES_AHEAD + 1))
@@ -97,20 +99,21 @@ def tile_nlgp_pb_t_kernel(tc, x, m, w_mask_words, w_mask_scales, out):
 
         x_images = []
 
-        def load_image(b):
-            x_image = x_pool.tile([P, PACK, PIXELS], BF16)
+        def load_images(first, count):
+            x_group = x_pool.tile([P, count, PACK, PIXELS], BF16, name="x_group_%d" % first)
             nc.sync.dma_start(
-                out=x_image[:].rearrange("p t n -> p (t n)"),
-                in_=x[b].rearrange("(p t) h w -> p (t h w)", t=PACK),
+                out=x_group[:].rearrange("p i t n -> p i (t n)"),
+                in_=x[first : first + count].rearrange("i (p t) h w -> p i (t h w)", t=PACK),
             )
-            x_images.append(x_image)
+            for i in range(count):
+                x_images.append(x_group[:, i])
 
         m_rows = keep.tile([IMAGES, PIXELS], BF16)
         nc.sync.dma_start(out=m_rows[:], in_=m)
-        load_image(0)
+        load_images(*LOADS[0])
         w_codes, w_scales = load_weight(nc, keep, w_mask_words, w_mask_scales)
-        for b in range(1, IMAGES):
-            load_image(b)
+        for first, count in LOADS[1:]:
+            load_images(first, count)
 
         identity = keep.tile([P, P], F32)
         make_identity(nc, identity[:])
@@ -163,7 +166,6 @@ def tile_nlgp_pb_t_kernel(tc, x, m, w_mask_words, w_mask_scales, out):
                 in_=products[b][:].rearrange("p n t -> p (n t)"),
             )
             last = b == IMAGES - 1
-            out_rows = out[b].rearrange("(m j) h w -> m j (h w)", j=OUT_BLOCKS)
             out_image = out_pool.tile([P, OUT_BLOCKS, PIXELS], F32)
             for block in range(OUT_BLOCKS):
                 d_cols = slice(block * P, (block + 1) * P)
@@ -177,11 +179,19 @@ def tile_nlgp_pb_t_kernel(tc, x, m, w_mask_words, w_mask_scales, out):
                     start=True,
                     stop=True,
                 )
-                if last:
-                    nc.vector.tensor_copy(out=out_image[:, block, :], in_=acc[:])
+                if last and block % 2 == 0:
+                    nc.vector.tensor_copy(out=out_image[:, block], in_=acc[:])
                 else:
-                    nc.scalar.copy(out=out_image[:, block, :], in_=acc[:])
-            nc.sync.dma_start(out=out_rows, in_=out_image[:])
+                    nc.scalar.copy(out=out_image[:, block], in_=acc[:])
+            out_rows = out[b].rearrange("(m j) h w -> m (j h w)", j=OUT_BLOCKS)
+            parts = LAST_STORES if last else 1
+            for columns in range(parts):
+                part = slice(
+                    columns * OUT_BLOCKS * PIXELS // parts, (columns + 1) * OUT_BLOCKS * PIXELS // parts
+                )
+                nc.sync.dma_start(
+                    out=out_rows[:, part], in_=out_image[:].rearrange("m j n -> m (j n)")[:, part]
+                )
 
         for b in range(GATES_AHEAD):
             spread_gate(b)

@@ -16,11 +16,12 @@ IMAGES = 16
 CHANNELS = P * PACK
 PIXELS = 512
 OUT_BLOCKS = CHANNELS // P
+WARM_UP_MATMULS = 8
 GATES_AHEAD = 3
 LOADS = [(0, 1), (1, 1), (2, 2), (4, 4), (8, 4), (12, 4)]
 LAST_STORES = 2
 RUN = 4
-GPSIMD_PIXELS = 96
+GPSIMD_PIXELS = 112
 VECTOR_PIXELS = PIXELS - GPSIMD_PIXELS
 
 FLOPS = 2 * IMAGES * CHANNELS * CHANNELS * PIXELS
@@ -56,17 +57,18 @@ def group_output_channels(nc, keep, w_codes, w_scales):
     return codes, scales
 
 
-def softmax_rows(nc, keep, m_rows):
-    attn = keep.tile([P, PIXELS], F32)
-    nc.vector.memset(attn[:], 0.0)
+def softmax_parts(nc, keep, identity, m_rows):
+    exps = keep.tile([P, PIXELS], F32)
+    nc.vector.memset(exps[:], 0.0)
+    selectors = keep.tile([P, IMAGES], F32)
+    nc.vector.memset(selectors[:], 0.0)
     row_max = keep.tile([IMAGES, 1], F32)
     nc.vector.reduce_max(out=row_max[:], in_=m_rows[:], axis=mybir.AxisListType.X)
     minus_max = keep.tile([IMAGES, 1], F32)
     nc.vector.tensor_scalar_mul(out=minus_max[:], in0=row_max[:], scalar1=-1.0)
-    exps = keep.tile([IMAGES, PIXELS], F32)
     exp_sum = keep.tile([IMAGES, 1], F32)
     nc.scalar.activation(
-        out=exps[:],
+        out=exps[0:IMAGES, :],
         in_=m_rows[:],
         func=mybir.ActivationFunctionType.Exp,
         bias=minus_max[:],
@@ -75,8 +77,10 @@ def softmax_rows(nc, keep, m_rows):
     )
     inv_sum = keep.tile([IMAGES, 1], F32)
     nc.vector.reciprocal(out=inv_sum[:], in_=exp_sum[:])
-    nc.vector.tensor_scalar_mul(out=attn[0:IMAGES, :], in0=exps[:], scalar1=inv_sum[:])
-    return attn
+    nc.vector.tensor_scalar_mul(
+        out=selectors[0:IMAGES, :], in0=identity[0:IMAGES, 0:IMAGES], scalar1=inv_sum[:]
+    )
+    return exps, selectors
 
 
 def tile_nlgp_pb_t_kernel(tc, x, m, w_mask_words, w_mask_scales, out):
@@ -115,10 +119,18 @@ def tile_nlgp_pb_t_kernel(tc, x, m, w_mask_words, w_mask_scales, out):
         for first, count in LOADS[1:]:
             load_images(first, count)
 
+        zeros = keep.tile([P, PIXELS], BF16)
+        nc.vector.memset(zeros[:], 0.0)
+        unused = gate_psum.tile([P, PIXELS], F32, name="gate")
+        for dummy in range(WARM_UP_MATMULS):
+            nc.tensor.matmul(
+                out=unused[:], lhsT=zeros[:, 0:P], rhs=zeros[:], start=True, stop=True
+            )
+
         identity = keep.tile([P, P], F32)
         make_identity(nc, identity[:])
         w_codes, w_scales = group_output_channels(nc, keep, w_codes, w_scales)
-        attn = softmax_rows(nc, keep, m_rows)
+        exps, selectors = softmax_parts(nc, keep, identity, m_rows)
 
         gates = {}
         gate_copies = {}
@@ -128,8 +140,8 @@ def tile_nlgp_pb_t_kernel(tc, x, m, w_mask_words, w_mask_scales, out):
             gate = gate_psum.tile([P, PIXELS], F32)
             nc.tensor.matmul(
                 out=gate[:],
-                lhsT=identity[:, b : b + 1].to_broadcast([P, P]),
-                rhs=attn[:],
+                lhsT=selectors[:, b : b + 1].to_broadcast([P, P]),
+                rhs=exps[:],
                 start=True,
                 stop=True,
             )

@@ -19,6 +19,7 @@ OUT_BLOCKS = CHANNELS // P
 WARM_UP_MATMULS = 8
 GATES_AHEAD = 3
 LOADS = [(0, 1), (1, 1), (2, 2), (4, 4), (8, 4), (12, 4)]
+DMA_ALIGN = 256
 LAST_STORES = 2
 RUN = 4
 GPSIMD_PIXELS = 112
@@ -28,7 +29,7 @@ FLOPS = 2 * IMAGES * CHANNELS * CHANNELS * PIXELS
 
 
 def load_weight(nc, keep, w_mask_words, w_mask_scales):
-    w_codes = keep.tile([P, CHANNELS], U32, align_bytes=64)
+    w_codes = keep.tile([P, CHANNELS], U32, align_bytes=DMA_ALIGN)
     w_scales = keep.tile([P, CHANNELS], U8, align_bytes=64)
     nc.vector.memset(w_scales[:].bitcast(I32), 0)
     for quadrant in range(4):
@@ -104,7 +105,9 @@ def tile_nlgp_pb_t_kernel(tc, x, m, w_mask_words, w_mask_scales, out):
         x_images = []
 
         def load_images(first, count):
-            x_group = x_pool.tile([P, count, PACK, PIXELS], BF16, name="x_group_%d" % first)
+            x_group = x_pool.tile(
+                [P, count, PACK, PIXELS], BF16, align_bytes=DMA_ALIGN, name="x_group_%d" % first
+            )
             nc.sync.dma_start(
                 out=x_group[:].rearrange("p i t n -> p i (t n)"),
                 in_=x[first : first + count].rearrange("i (p t) h w -> p i (t h w)", t=PACK),
@@ -178,7 +181,7 @@ def tile_nlgp_pb_t_kernel(tc, x, m, w_mask_words, w_mask_scales, out):
                 in_=products[b][:].rearrange("p n t -> p (n t)"),
             )
             last = b == IMAGES - 1
-            out_image = out_pool.tile([P, OUT_BLOCKS, PIXELS], F32)
+            out_image = out_pool.tile([P, OUT_BLOCKS, PIXELS], F32, align_bytes=DMA_ALIGN)
             for block in range(OUT_BLOCKS):
                 d_cols = slice(block * P, (block + 1) * P)
                 acc = acc_psum.tile([P, PIXELS], F32)

@@ -20,7 +20,6 @@ WARM_UP_MATMULS = 8
 GATES_AHEAD = 3
 LOADS = [(0, 1), (1, 1), (2, 2), (4, 4), (8, 4), (12, 4)]
 DMA_ALIGN = 256
-LAST_STORES = 2
 RUN = 4
 GPSIMD_PIXELS = 112
 VECTOR_PIXELS = PIXELS - GPSIMD_PIXELS
@@ -44,18 +43,11 @@ def load_weight(nc, keep, w_mask_words, w_mask_scales):
     return w_codes, w_scales
 
 
-def group_output_channels(nc, keep, w_codes, w_scales):
-    codes = keep.tile([P, CHANNELS], U32, align_bytes=64)
-    scales = keep.tile([P, CHANNELS], U8, align_bytes=64)
-    nc.gpsimd.tensor_copy(
-        out=codes[:].rearrange("p (j m) -> p m j", j=OUT_BLOCKS),
-        in_=w_codes[:].rearrange("p (m j) -> p m j", j=OUT_BLOCKS),
+def group_output_channels(nc, grouped, arrived):
+    nc.vector.tensor_copy(
+        out=grouped.rearrange("p (j m) -> p j m", j=OUT_BLOCKS),
+        in_=arrived.rearrange("p (m j) -> p j m", j=OUT_BLOCKS),
     )
-    nc.gpsimd.tensor_copy(
-        out=scales[:].rearrange("p (j m) -> p m j", j=OUT_BLOCKS),
-        in_=w_scales[:].rearrange("p (m j) -> p m j", j=OUT_BLOCKS),
-    )
-    return codes, scales
 
 
 def softmax_parts(nc, keep, identity, m_rows):
@@ -118,7 +110,7 @@ def tile_nlgp_pb_t_kernel(tc, x, m, w_mask_words, w_mask_scales, out):
         m_rows = keep.tile([IMAGES, PIXELS], BF16)
         nc.sync.dma_start(out=m_rows[:], in_=m)
         load_images(*LOADS[0])
-        w_codes, w_scales = load_weight(nc, keep, w_mask_words, w_mask_scales)
+        arrived_codes, arrived_scales = load_weight(nc, keep, w_mask_words, w_mask_scales)
         for first, count in LOADS[1:]:
             load_images(first, count)
 
@@ -132,8 +124,9 @@ def tile_nlgp_pb_t_kernel(tc, x, m, w_mask_words, w_mask_scales, out):
 
         identity = keep.tile([P, P], F32)
         make_identity(nc, identity[:])
-        w_codes, w_scales = group_output_channels(nc, keep, w_codes, w_scales)
         exps, selectors = softmax_parts(nc, keep, identity, m_rows)
+        w_codes = keep.tile([P, CHANNELS], U32, align_bytes=64, name="grouped_codes")
+        w_scales = keep.tile([P, CHANNELS], U8, align_bytes=64, name="grouped_scales")
 
         gates = {}
         gate_copies = {}
@@ -199,18 +192,13 @@ def tile_nlgp_pb_t_kernel(tc, x, m, w_mask_words, w_mask_scales, out):
                 else:
                     nc.scalar.copy(out=out_image[:, block], in_=acc[:])
             out_rows = out[b].rearrange("(m j) h w -> m (j h w)", j=OUT_BLOCKS)
-            parts = LAST_STORES if last else 1
-            for columns in range(parts):
-                part = slice(
-                    columns * OUT_BLOCKS * PIXELS // parts, (columns + 1) * OUT_BLOCKS * PIXELS // parts
-                )
-                nc.sync.dma_start(
-                    out=out_rows[:, part], in_=out_image[:].rearrange("m j n -> m (j n)")[:, part]
-                )
+            nc.sync.dma_start(out=out_rows, in_=out_image[:].rearrange("m j n -> m (j n)"))
 
         for b in range(GATES_AHEAD):
             spread_gate(b)
+        group_output_channels(nc, w_codes[:].bitcast(I32), arrived_codes[:].bitcast(I32))
         multiply(0)
+        group_output_channels(nc, w_scales[:], arrived_scales[:])
         for b in range(IMAGES):
             if b + GATES_AHEAD < IMAGES:
                 spread_gate(b + GATES_AHEAD)

@@ -17,6 +17,7 @@ CHANNELS = P * PACK
 PIXELS = 512
 OUT_BLOCKS = CHANNELS // P
 WARM_UP_MATMULS = 8
+FIRST_GATE_PIECES = 2
 GATES_AHEAD = 3
 LOADS = [(0, 1), (1, 1), (2, 2), (4, 4), (8, 4), (12, 4)]
 DMA_ALIGN = 256
@@ -43,8 +44,8 @@ def load_weight(nc, keep, w_mask_words, w_mask_scales):
     return w_codes, w_scales
 
 
-def group_output_channels(nc, grouped, arrived):
-    nc.vector.tensor_copy(
+def group_output_channels(engine, grouped, arrived):
+    engine.tensor_copy(
         out=grouped.rearrange("p (j m) -> p j m", j=OUT_BLOCKS),
         in_=arrived.rearrange("p (m j) -> p j m", j=OUT_BLOCKS),
     )
@@ -131,32 +132,41 @@ def tile_nlgp_pb_t_kernel(tc, x, m, w_mask_words, w_mask_scales, out):
         gates = {}
         gate_copies = {}
         products = {}
+        quantized = {}
 
         def spread_gate(b):
-            gate = gate_psum.tile([P, PIXELS], F32)
-            nc.tensor.matmul(
-                out=gate[:],
-                lhsT=selectors[:, b : b + 1].to_broadcast([P, P]),
-                rhs=exps[:],
-                start=True,
-                stop=True,
-            )
-            gates[b] = gate
+            pieces = FIRST_GATE_PIECES if b == 0 else 1
+            width = PIXELS // pieces
+            gates[b] = []
+            for piece in range(pieces):
+                gate = gate_psum.tile([P, width], F32)
+                nc.tensor.matmul(
+                    out=gate[:],
+                    lhsT=selectors[:, b : b + 1].to_broadcast([P, P]),
+                    rhs=exps[:, piece * width : (piece + 1) * width],
+                    start=True,
+                    stop=True,
+                )
+                gates[b].append(gate)
             gate_copy = gate_pool.tile([P, GPSIMD_PIXELS], F32)
-            nc.scalar.copy(out=gate_copy[:], in_=gate[:, VECTOR_PIXELS:PIXELS])
+            nc.scalar.copy(out=gate_copy[:], in_=gates[b][-1][:, width - GPSIMD_PIXELS : width])
             gate_copies[b] = gate_copy
 
         def multiply(b):
             y = y_pool.tile([P, PIXELS, PACK], BF16, align_bytes=64)
-            nc.vector.tensor_tensor(
-                out=y[:, 0:VECTOR_PIXELS, :].rearrange("p (c i) t -> p c t i", i=RUN),
-                in0=x_images[b][:, :, 0:VECTOR_PIXELS].rearrange("p t (c i) -> p c t i", i=RUN),
-                in1=gates[b][:, 0:VECTOR_PIXELS]
-                .rearrange("p (c i) -> p c i", i=RUN)
-                .unsqueeze(2)
-                .to_broadcast([P, VECTOR_PIXELS // RUN, PACK, RUN]),
-                op=mybir.AluOpType.mult,
-            )
+            width = PIXELS // len(gates[b])
+            for piece, gate in enumerate(gates[b]):
+                first = piece * width
+                stop = min(first + width, VECTOR_PIXELS)
+                nc.vector.tensor_tensor(
+                    out=y[:, first:stop, :].rearrange("p (c i) t -> p c t i", i=RUN),
+                    in0=x_images[b][:, :, first:stop].rearrange("p t (c i) -> p c t i", i=RUN),
+                    in1=gate[:, 0 : stop - first]
+                    .rearrange("p (c i) -> p c i", i=RUN)
+                    .unsqueeze(2)
+                    .to_broadcast([P, (stop - first) // RUN, PACK, RUN]),
+                    op=mybir.AluOpType.mult,
+                )
             nc.gpsimd.tensor_tensor(
                 out=y[:, VECTOR_PIXELS:PIXELS, :],
                 in0=x_images[b][:, :, VECTOR_PIXELS:PIXELS].rearrange("p t n -> p n t"),
@@ -165,7 +175,7 @@ def tile_nlgp_pb_t_kernel(tc, x, m, w_mask_words, w_mask_scales, out):
             )
             products[b] = y
 
-        def convolve(b):
+        def quantize(b):
             y_codes = y_pool.tile([P, PIXELS], U32, align_bytes=64)
             y_scales = y_pool.tile([P, PIXELS], U8, align_bytes=64)
             nc.vector.quantize_mx(
@@ -173,7 +183,11 @@ def tile_nlgp_pb_t_kernel(tc, x, m, w_mask_words, w_mask_scales, out):
                 scales=y_scales[:],
                 in_=products[b][:].rearrange("p n t -> p (n t)"),
             )
-            last = b == IMAGES - 1
+            quantized[b] = (y_codes, y_scales)
+
+        def convolve(b):
+            y_codes, y_scales = quantized[b]
+            shared = b >= IMAGES - 2
             out_image = out_pool.tile([P, OUT_BLOCKS, PIXELS], F32, align_bytes=DMA_ALIGN)
             for block in range(OUT_BLOCKS):
                 d_cols = slice(block * P, (block + 1) * P)
@@ -187,7 +201,7 @@ def tile_nlgp_pb_t_kernel(tc, x, m, w_mask_words, w_mask_scales, out):
                     start=True,
                     stop=True,
                 )
-                if last and block % 2 == 0:
+                if shared and block % 2 == 0:
                     nc.vector.tensor_copy(out=out_image[:, block], in_=acc[:])
                 else:
                     nc.scalar.copy(out=out_image[:, block], in_=acc[:])
@@ -196,12 +210,16 @@ def tile_nlgp_pb_t_kernel(tc, x, m, w_mask_words, w_mask_scales, out):
 
         for b in range(GATES_AHEAD):
             spread_gate(b)
-        group_output_channels(nc, w_codes[:].bitcast(I32), arrived_codes[:].bitcast(I32))
+        group_output_channels(nc.vector, w_codes[:].bitcast(I32), arrived_codes[:].bitcast(I32))
+        group_output_channels(nc.gpsimd, w_scales[:], arrived_scales[:])
         multiply(0)
-        group_output_channels(nc, w_scales[:], arrived_scales[:])
         for b in range(IMAGES):
             if b + GATES_AHEAD < IMAGES:
                 spread_gate(b + GATES_AHEAD)
             if b + 1 < IMAGES:
                 multiply(b + 1)
+            if b < IMAGES - 1:
+                quantize(b)
+            if b == IMAGES - 2:
+                quantize(b + 1)
             convolve(b)

from contextlib import ExitStack

import concourse.mybir as mybir
from concourse.masks import make_identity

F32 = mybir.dt.float32
BF16 = mybir.dt.bfloat16
I32 = mybir.dt.int32
U32 = mybir.dt.uint32
U8 = mybir.dt.uint8
FP8X4 = mybir.dt.float8_e4m3fn_x4

P = 128
PACK = 4
IMAGES = 16
CHANNELS = P * PACK
PIXELS = 512
OUT_BLOCKS = CHANNELS // P
WARM_UP_MATMULS = 8
FIRST_GATE_PIECES = 2
GATES_AHEAD = 3
LOADS = [(0, 1), (1, 1), (2, 2), (4, 4), (8, 4), (12, 4)]
DMA_ALIGN = 256
RUN = 4
GPSIMD_PIXELS = 112
VECTOR_PIXELS = PIXELS - GPSIMD_PIXELS

FLOPS = 2 * IMAGES * CHANNELS * CHANNELS * PIXELS


def load_weight(nc, keep, w_mask_words, w_mask_scales):
    w_codes = keep.tile([P, CHANNELS], U32, align_bytes=DMA_ALIGN)
    w_scales = keep.tile([P, CHANNELS], U8, align_bytes=64)
    nc.vector.memset(w_scales[:].bitcast(I32), 0)
    for quadrant in range(4):
        nc.scalar.dma_start(
            out=w_scales[32 * quadrant : 32 * quadrant + 4, :].bitcast(I32),
            in_=w_mask_scales[0, 4 * quadrant : 4 * quadrant + 4, :].bitcast(I32),
        )
    nc.sync.dma_start(
        out=w_codes[:].bitcast(I32),
        in_=w_mask_words[0].rearrange("p n t -> p (n t)").bitcast(I32),
    )
    return w_codes, w_scales


def group_output_channels(engine, grouped, arrived):
    engine.tensor_copy(
        out=grouped.rearrange("p (j m) -> p j m", j=OUT_BLOCKS),
        in_=arrived.rearrange("p (m j) -> p j m", j=OUT_BLOCKS),
    )


def softmax_parts(nc, keep, identity, m_rows):
    exps = keep.tile([P, PIXELS], F32)
    nc.vector.memset(exps[:], 0.0)
    selectors = keep.tile([P, IMAGES], F32)
    nc.vector.memset(selectors[:], 0.0)
    row_max = keep.tile([IMAGES, 1], F32)
    nc.vector.reduce_max(out=row_max[:], in_=m_rows[:], axis=mybir.AxisListType.X)
    minus_max = keep.tile([IMAGES, 1], F32)
    nc.vector.tensor_scalar_mul(out=minus_max[:], in0=row_max[:], scalar1=-1.0)
    exp_sum = keep.tile([IMAGES, 1], F32)
    nc.scalar.activation(
        out=exps[0:IMAGES, :],
        in_=m_rows[:],
        func=mybir.ActivationFunctionType.Exp,
        bias=minus_max[:],
        scale=1.0,
        accum_out=exp_sum[:],
    )
    inv_sum = keep.tile([IMAGES, 1], F32)
    nc.vector.reciprocal(out=inv_sum[:], in_=exp_sum[:])
    nc.vector.tensor_scalar_mul(
        out=selectors[0:IMAGES, :], in0=identity[0:IMAGES, 0:IMAGES], scalar1=inv_sum[:]
    )
    return exps, selectors


def tile_nlgp_pb_t_kernel(tc, x, m, w_mask_words, w_mask_scales, out):
    nc = tc.nc
    with ExitStack() as ctx:
        ctx.enter_context(tc.manual_schedule())
        keep = ctx.enter_context(tc.tile_pool(name="keep", bufs=1))
        x_pool = ctx.enter_context(tc.tile_pool(name="x_pool", bufs=1))
        y_pool = ctx.enter_context(tc.tile_pool(name="y_pool", bufs=3))
        out_pool = ctx.enter_context(tc.tile_pool(name="out_pool", bufs=IMAGES))
        gate_pool = ctx.enter_context(tc.tile_pool(name="gate_pool", bufs=GATES_AHEAD + 1))
        gate_psum = ctx.enter_context(tc.psum_pool(name="gate_psum", bufs=GATES_AHEAD))
        acc_psum = ctx.enter_context(tc.psum_pool(name="acc_psum", bufs=8 - GATES_AHEAD))

        scratch = keep.tile([P, 2], F32)
        nc.vector.memset(scratch[:], 0.0)
        nc.scalar.activation(
            out=scratch[:, 1:2], in_=scratch[:, 0:1], func=mybir.ActivationFunctionType.Exp
        )

        x_images = []

        def load_images(first, count):
            x_group = x_pool.tile(
                [P, count, PACK, PIXELS], BF16, align_bytes=DMA_ALIGN, name="x_group_%d" % first
            )
            nc.sync.dma_start(
                out=x_group[:].rearrange("p i t n -> p i (t n)"),
                in_=x[first : first + count].rearrange("i (p t) h w -> p i (t h w)", t=PACK),
            )
            for i in range(count):
                x_images.append(x_group[:, i])

        m_rows = keep.tile([IMAGES, PIXELS], BF16)
        nc.sync.dma_start(out=m_rows[:], in_=m)
        load_images(*LOADS[0])
        arrived_codes, arrived_scales = load_weight(nc, keep, w_mask_words, w_mask_scales)
        for first, count in LOADS[1:]:
            load_images(first, count)

        zeros = keep.tile([P, PIXELS], BF16)
        nc.vector.memset(zeros[:], 0.0)
        unused = gate_psum.tile([P, PIXELS], F32, name="gate")
        for dummy in range(WARM_UP_MATMULS):
            nc.tensor.matmul(
                out=unused[:], lhsT=zeros[:, 0:P], rhs=zeros[:], start=True, stop=True
            )

        identity = keep.tile([P, P], F32)
        make_identity(nc, identity[:])
        exps, selectors = softmax_parts(nc, keep, identity, m_rows)
        w_codes = keep.tile([P, CHANNELS], U32, align_bytes=64, name="grouped_codes")
        w_scales = keep.tile([P, CHANNELS], U8, align_bytes=64, name="grouped_scales")

        gates = {}
        gate_copies = {}
        products = {}
        quantized = {}

        def spread_gate(b):
            pieces = FIRST_GATE_PIECES if b == 0 else 1
            width = PIXELS // pieces
            gates[b] = []
            for piece in range(pieces):
                gate = gate_psum.tile([P, width], F32)
                nc.tensor.matmul(
                    out=gate[:],
                    lhsT=selectors[:, b : b + 1].to_broadcast([P, P]),
                    rhs=exps[:, piece * width : (piece + 1) * width],
                    start=True,
                    stop=True,
                )
                gates[b].append(gate)
            gate_copy = gate_pool.tile([P, GPSIMD_PIXELS], F32)
            nc.scalar.copy(out=gate_copy[:], in_=gates[b][-1][:, width - GPSIMD_PIXELS : width])
            gate_copies[b] = gate_copy

        def multiply(b):
            y = y_pool.tile([P, PIXELS, PACK], BF16, align_bytes=64)
            width = PIXELS // len(gates[b])
            for piece, gate in enumerate(gates[b]):
                first = piece * width
                stop = min(first + width, VECTOR_PIXELS)
                nc.vector.tensor_tensor(
                    out=y[:, first:stop, :].rearrange("p (c i) t -> p c t i", i=RUN),
                    in0=x_images[b][:, :, first:stop].rearrange("p t (c i) -> p c t i", i=RUN),
                    in1=gate[:, 0 : stop - first]
                    .rearrange("p (c i) -> p c i", i=RUN)
                    .unsqueeze(2)
                    .to_broadcast([P, (stop - first) // RUN, PACK, RUN]),
                    op=mybir.AluOpType.mult,
                )
            nc.gpsimd.tensor_tensor(
                out=y[:, VECTOR_PIXELS:PIXELS, :],
                in0=x_images[b][:, :, VECTOR_PIXELS:PIXELS].rearrange("p t n -> p n t"),
                in1=gate_copies[b][:].unsqueeze(2).to_broadcast([P, GPSIMD_PIXELS, PACK]),
                op=mybir.AluOpType.mult,
            )
            products[b] = y

        def quantize(b):
            y_codes = y_pool.tile([P, PIXELS], U32, align_bytes=64)
            y_scales = y_pool.tile([P, PIXELS], U8, align_bytes=64)
            nc.vector.quantize_mx(
                out=y_codes[:].bitcast(FP8X4),
                scales=y_scales[:],
                in_=products[b][:].rearrange("p n t -> p (n t)"),
            )
            quantized[b] = (y_codes, y_scales)

        def convolve(b):
            y_codes, y_scales = quantized[b]
            shared = b >= IMAGES - 2
            out_image = out_pool.tile([P, OUT_BLOCKS, PIXELS], F32, align_bytes=DMA_ALIGN)
            for block in range(OUT_BLOCKS):
                d_cols = slice(block * P, (block + 1) * P)
                acc = acc_psum.tile([P, PIXELS], F32)
                nc.tensor.matmul_mx(
                    out=acc[:],
                    lhsT=w_codes[:, d_cols].bitcast(FP8X4),
                    lhsT_scale=w_scales[:, d_cols],
                    rhs=y_codes[:].bitcast(FP8X4),
                    rhs_scale=y_scales[:],
                    start=True,
                    stop=True,
                )
                if shared and block % 2 == 0:
                    nc.vector.tensor_copy(out=out_image[:, block], in_=acc[:])
                else:
                    nc.scalar.copy(out=out_image[:, block], in_=acc[:])
            out_rows = out[b].rearrange("(m j) h w -> m (j h w)", j=OUT_BLOCKS)
            nc.sync.dma_start(out=out_rows, in_=out_image[:].rearrange("m j n -> m (j n)"))

        for b in range(GATES_AHEAD):
            spread_gate(b)
        group_output_channels(nc.vector, w_codes[:].bitcast(I32), arrived_codes[:].bitcast(I32))
        group_output_channels(nc.gpsimd, w_scales[:], arrived_scales[:])
        multiply(0)
        for b in range(IMAGES):
            if b + GATES_AHEAD < IMAGES:
                spread_gate(b + GATES_AHEAD)
            if b + 1 < IMAGES:
                multiply(b + 1)
            if b < IMAGES - 1:
                quantize(b)
            if b == IMAGES - 2:
                quantize(b + 1)
            convolve(b)
